import numpy as np
import ml_dtypes


def mxq(x, axis, fmt="e4m3"):
    dtype, down = {"e4m3": (ml_dtypes.float8_e4m3fn, 7), "e5m2": (ml_dtypes.float8_e5m2, 14)}[fmt]
    v = np.moveaxis(np.asarray(x, np.float32).astype(ml_dtypes.bfloat16).astype(np.float64), axis, -1)
    blocks = v.reshape(v.shape[:-1] + (-1, 32))
    amax = np.abs(blocks).max(-1, keepdims=True)
    byte = np.maximum(np.where(amax > 0, np.frexp(amax)[1] - 1 + 127, 0) - down, 1)
    scale = np.exp2(byte - 127.0)
    codes = (blocks / scale).astype(np.float32).astype(dtype).astype(np.float64)
    return np.moveaxis((codes * scale).reshape(v.shape), -1, axis)


WIDE = False


def mx_kscale(k):
    if not WIDE:
        return np.ones(k)
    levels = np.array([20, -20, 10, -10, 0])
    a = np.random.permutation(np.resize(levels, k // 512 * 4)).reshape(k // 512, 4)
    idx = np.arange(k)
    return np.exp2(a[idx // 512, idx % 128 // 32])


BF16 = ml_dtypes.bfloat16


def bf(x):
    return np.asarray(x, np.float32).astype(BF16)


def f64(x):
    return np.asarray(x).astype(np.float64)


B, N, D, H, K = 8, 64, 512, 512, 512
NT = B * N
LN2PI_2 = np.log(2.0 * np.pi) / 2.0


def setup_inputs():
    s = mx_kscale(K)
    cent = 0.4 * np.random.standard_normal((B, D))
    idx = np.random.randint(0, B, K)
    xf = np.repeat(cent, N, axis=0) + 0.5 * np.random.standard_normal((NT, D))
    mean = 0.6 * cent[idx] + 0.1 * np.random.standard_normal((K, D))
    var = 0.35 * np.exp(0.2 * np.random.standard_normal((K, D))) * s[:, None]
    g = np.random.standard_normal((NT, K)) * np.exp2(np.random.randint(-12, 1, (NT, 1))) * s[None, :]
    return {"xf": bf(xf), "mean": bf(mean), "var": bf(var), "grad_out": bf(g)}


def reference(xf, mean, var, grad_out):
    xv, mv, vv = f64(xf), f64(mean), f64(var)
    inv_var = 1.0 / vv
    gq = mxq(f64(grad_out), 1, "e5m2")
    a = gq @ mxq(mv * inv_var, 0, "e4m3")
    b = gq @ mxq(inv_var, 0, "e4m3")
    return a - xv * b

@@ -1,0 +1,150 @@
+from contextlib import ExitStack
+
+import concourse.masks as masks
+import concourse.mybir as mybir
+
+F32 = mybir.dt.float32
+BF16 = mybir.dt.bfloat16
+U32 = mybir.dt.uint32
+U8 = mybir.dt.uint8
+E4M3_X4 = mybir.dt.float8_e4m3fn_x4
+E5M2_X4 = mybir.dt.float8_e5m2_x4
+ACT = mybir.ActivationFunctionType
+ALU = mybir.AluOpType
+
+P = 128
+PACK = 4
+K = P * PACK
+NT = 512
+D = 512
+ROW_TILES = NT // P
+HALF_K = K // 2
+COL_CHUNK = 128
+COL_CHUNKS = D // COL_CHUNK
+RUN = 4
+
+FLOPS = 2 * 2 * NT * K * D
+
+
+def load_k_rows(nc, rows_sb, rows):
+    for u in range(2):
+        nc.sync.dma_start(
+            out=rows_sb[:, 2 * u : 2 * u + 2, :],
+            in_=rows[HALF_K * u : HALF_K * (u + 1), :].rearrange("(p e) d -> p e d", e=2),
+        )
+
+
+def by_row(plane_major, cols):
+    return plane_major[:, :, cols].rearrange("p t (c i) -> p c t i", i=RUN)
+
+
+def by_word(grouped, cols):
+    return grouped[:, cols, :].rearrange("p (c i) t -> p c t i", i=RUN)
+
+
+def tile_gaussianmlpbasislayer_pb_s_kernel(tc, xf, mean, var, grad_out, out):
+    nc = tc.nc
+    with ExitStack() as ctx:
+        keep = ctx.enter_context(tc.tile_pool(name="keep", bufs=1))
+        products = ctx.enter_context(tc.tile_pool(name="products", bufs=ROW_TILES))
+        psum_t = ctx.enter_context(tc.psum_pool(name="psum_t", bufs=2))
+        psum_mm = ctx.enter_context(tc.psum_pool(name="psum_mm", bufs=3))
+
+        var_sb = keep.tile([P, PACK, D], BF16)
+        load_k_rows(nc, var_sb, var)
+        g_sb = keep.tile([P, ROW_TILES, K], BF16)
+        nc.sync.dma_start(out=g_sb[:], in_=grad_out.rearrange("(p i) k -> p i k", i=ROW_TILES))
+        mean_sb = keep.tile([P, PACK, D], BF16)
+        load_k_rows(nc, mean_sb, mean)
+        xf_sb = keep.tile([P, ROW_TILES, D], BF16)
+        nc.sync.dma_start(out=xf_sb[:], in_=xf.rearrange("(p i) d -> p i d", i=ROW_TILES))
+
+        identity = keep.tile([P, P], F32)
+        masks.make_identity(nc, identity[:])
+
+        rsqrt = keep.tile([P, PACK, D], F32)
+        guess = keep.tile([P, PACK, D], F32)
+        minus_vs = keep.tile([P, PACK, D], F32)
+        inv_var = keep.tile([P, PACK, D], F32)
+        for t in range(PACK):
+            nc.scalar.activation(out=rsqrt[:, t, :], in_=var_sb[:, t, :], func=ACT.Abs_reciprocal_sqrt)
+            nc.scalar.activation(out=guess[:, t, :], in_=rsqrt[:, t, :], func=ACT.Square)
+            nc.vector.scalar_tensor_tensor(
+                out=minus_vs[:, t, :], in0=guess[:, t, :], scalar=-1.0, in1=var_sb[:, t, :],
+                op0=ALU.mult, op1=ALU.mult,
+            )
+            nc.vector.scalar_tensor_tensor(
+                out=inv_var[:, t, :], in0=minus_vs[:, t, :], scalar=2.0, in1=guess[:, t, :],
+                op0=ALU.add, op1=ALU.mult,
+            )
+
+        g_grouped = keep.tile([P, ROW_TILES, P, 2], F32, align_bytes=64)
+        for pair in range(ROW_TILES // 2):
+            g_t = psum_t.tile([P, 2, 2, P], F32)
+            for j in range(2):
+                g_words = g_sb[:, 2 * pair + j, :].bitcast(F32)
+                for u in range(2):
+                    nc.tensor.transpose(g_t[:, j, u, :], g_words[:, P * u : P * (u + 1)], identity[:])
+            nc.scalar.copy(
+                out=g_grouped[:, 2 * pair : 2 * pair + 2, :, :],
+                in_=g_t[:].rearrange("p j u n -> p j n u"),
+            )
+        g_codes = keep.tile([P, NT], U32, align_bytes=64)
+        g_scales = keep.tile([P, NT], U8, align_bytes=64)
+        nc.vector.quantize_mx(
+            out=g_codes[:].bitcast(E5M2_X4),
+            scales=g_scales[:],
+            in_=g_grouped[:].rearrange("p i n u -> p (i n u)").bitcast(BF16),
+        )
+
+        iv_grouped = keep.tile([P, D, PACK], BF16, align_bytes=64)
+        miv_grouped = keep.tile([P, D, PACK], BF16, align_bytes=64)
+        iv_codes = keep.tile([P, D], U32, align_bytes=64)
+        iv_scales = keep.tile([P, D], U8, align_bytes=64)
+        miv_codes = keep.tile([P, D], U32, align_bytes=64)
+        miv_scales = keep.tile([P, D], U8, align_bytes=64)
+        for c in range(COL_CHUNKS):
+            cols = slice(COL_CHUNK * c, COL_CHUNK * (c + 1))
+            nc.scalar.copy(out=by_word(iv_grouped, cols), in_=by_row(inv_var, cols))
+            nc.vector.tensor_tensor(
+                out=by_word(miv_grouped, cols), in0=by_row(mean_sb, cols), in1=by_row(inv_var, cols),
+                op=ALU.mult,
+            )
+        nc.vector.quantize_mx(
+            out=iv_codes[:].bitcast(E4M3_X4),
+            scales=iv_scales[:],
+            in_=iv_grouped[:].rearrange("p w t -> p (w t)"),
+        )
+        nc.vector.quantize_mx(
+            out=miv_codes[:].bitcast(E4M3_X4),
+            scales=miv_scales[:],
+            in_=miv_grouped[:].rearrange("p w t -> p (w t)"),
+        )
+
+        xf_b = []
+        for i in range(ROW_TILES):
+            rows = slice(P * i, P * (i + 1))
+            b_ps = psum_mm.tile([P, D], F32)
+            nc.tensor.matmul_mx(
+                out=b_ps[:],
+                lhsT=g_codes[:, rows].bitcast(E5M2_X4), lhsT_scale=g_scales[:, rows],
+                rhs=iv_codes[:].bitcast(E4M3_X4), rhs_scale=iv_scales[:],
+                start=True, stop=True,
+            )
+            product = products.tile([P, D], F32)
+            nc.vector.tensor_tensor(out=product[:], in0=b_ps[:], in1=xf_sb[:, i, :], op=ALU.mult)
+            xf_b.append(product)
+
+        out_sb = keep.tile([P, ROW_TILES, D], F32)
+        out_rows = out.rearrange("(p i) d -> p i d", i=ROW_TILES)
+        for i in range(ROW_TILES):
+            rows = slice(P * i, P * (i + 1))
+            a_ps = psum_mm.tile([P, D], F32)
+            nc.tensor.matmul_mx(
+                out=a_ps[:],
+                lhsT=g_codes[:, rows].bitcast(E5M2_X4), lhsT_scale=g_scales[:, rows],
+                rhs=miv_codes[:].bitcast(E4M3_X4), rhs_scale=miv_scales[:],
+                start=True, stop=True,
+            )
+            nc.vector.tensor_tensor(out=out_sb[:, i, :], in0=a_ps[:], in1=xf_b[i][:], op=ALU.subtract)
+            nc.sync.dma_start(out=out_rows[:, i, :], in_=out_sb[:, i, :])

@@ -19,9 +19,11 @@ NT = 512
 D = 512
 ROW_TILES = NT // P
 HALF_K = K // 2
-COL_CHUNK = 128
+PSUM_BANKS = 8
+COL_CHUNK = 64
 COL_CHUNKS = D // COL_CHUNK
 RUN = 4
+LAG = 2
 
 FLOPS = 2 * 2 * NT * K * D
 
@@ -34,12 +36,24 @@ def load_k_rows(nc, rows_sb, rows):
         )
 
 
-def by_row(plane_major, cols):
-    return plane_major[:, :, cols].rearrange("p t (c i) -> p c t i", i=RUN)
+def chunk_cols(c):
+    return slice(COL_CHUNK * c, COL_CHUNK * (c + 1))
 
 
-def by_word(grouped, cols):
-    return grouped[:, cols, :].rearrange("p (c i) t -> p c t i", i=RUN)
+def by_row(plane_major, c):
+    return plane_major[:, :, chunk_cols(c)].rearrange("p t (g i) -> p g t i", i=RUN)
+
+
+def by_word(grouped, c):
+    return grouped[:, chunk_cols(c), :].rearrange("p (g i) t -> p g t i", i=RUN)
+
+
+def quantise_chunk(nc, grouped, codes, scales, c):
+    nc.vector.quantize_mx(
+        out=codes[:, chunk_cols(c)].bitcast(E4M3_X4),
+        scales=scales[:, chunk_cols(c)],
+        in_=grouped[:, chunk_cols(c), :].rearrange("p w t -> p (w t)"),
+    )
 
 
 def tile_gaussianmlpbasislayer_pb_s_kernel(tc, xf, mean, var, grad_out, out):
@@ -47,15 +61,15 @@ def tile_gaussianmlpbasislayer_pb_s_kernel(tc, xf, mean, var, grad_out, out):
     with ExitStack() as ctx:
         keep = ctx.enter_context(tc.tile_pool(name="keep", bufs=1))
         products = ctx.enter_context(tc.tile_pool(name="products", bufs=ROW_TILES))
-        psum_t = ctx.enter_context(tc.psum_pool(name="psum_t", bufs=2))
-        psum_mm = ctx.enter_context(tc.psum_pool(name="psum_mm", bufs=3))
+        psum = ctx.enter_context(tc.psum_pool(name="psum", bufs=PSUM_BANKS))
+        ctx.enter_context(tc.manual_schedule())
 
         var_sb = keep.tile([P, PACK, D], BF16)
         load_k_rows(nc, var_sb, var)
-        g_sb = keep.tile([P, ROW_TILES, K], BF16)
-        nc.sync.dma_start(out=g_sb[:], in_=grad_out.rearrange("(p i) k -> p i k", i=ROW_TILES))
         mean_sb = keep.tile([P, PACK, D], BF16)
         load_k_rows(nc, mean_sb, mean)
+        g_sb = keep.tile([P, ROW_TILES, K], BF16)
+        nc.sync.dma_start(out=g_sb[:], in_=grad_out.rearrange("(p i) k -> p i k", i=ROW_TILES))
         xf_sb = keep.tile([P, ROW_TILES, D], BF16)
         nc.sync.dma_start(out=xf_sb[:], in_=xf.rearrange("(p i) d -> p i d", i=ROW_TILES))
 
@@ -63,24 +77,20 @@ def tile_gaussianmlpbasislayer_pb_s_kernel(tc, xf, mean, var, grad_out, out):
         masks.make_identity(nc, identity[:])
 
         rsqrt = keep.tile([P, PACK, D], F32)
-        guess = keep.tile([P, PACK, D], F32)
-        minus_vs = keep.tile([P, PACK, D], F32)
         inv_var = keep.tile([P, PACK, D], F32)
-        for t in range(PACK):
-            nc.scalar.activation(out=rsqrt[:, t, :], in_=var_sb[:, t, :], func=ACT.Abs_reciprocal_sqrt)
-            nc.scalar.activation(out=guess[:, t, :], in_=rsqrt[:, t, :], func=ACT.Square)
-            nc.vector.scalar_tensor_tensor(
-                out=minus_vs[:, t, :], in0=guess[:, t, :], scalar=-1.0, in1=var_sb[:, t, :],
-                op0=ALU.mult, op1=ALU.mult,
-            )
-            nc.vector.scalar_tensor_tensor(
-                out=inv_var[:, t, :], in0=minus_vs[:, t, :], scalar=2.0, in1=guess[:, t, :],
-                op0=ALU.add, op1=ALU.mult,
-            )
+        for step in range(COL_CHUNKS + 1):
+            if step < COL_CHUNKS:
+                cols = chunk_cols(step)
+                nc.scalar.activation(
+                    out=rsqrt[:, :, cols], in_=var_sb[:, :, cols], func=ACT.Abs_reciprocal_sqrt
+                )
+            if step >= 1:
+                cols = chunk_cols(step - 1)
+                nc.scalar.activation(out=inv_var[:, :, cols], in_=rsqrt[:, :, cols], func=ACT.Square)
 
         g_grouped = keep.tile([P, ROW_TILES, P, 2], F32, align_bytes=64)
         for pair in range(ROW_TILES // 2):
-            g_t = psum_t.tile([P, 2, 2, P], F32)
+            g_t = psum.tile([P, 2, 2, P], F32, tag="bank")
             for j in range(2):
                 g_words = g_sb[:, 2 * pair + j, :].bitcast(F32)
                 for u in range(2):
@@ -89,13 +99,6 @@ def tile_gaussianmlpbasislayer_pb_s_kernel(tc, xf, mean, var, grad_out, out):
                 out=g_grouped[:, 2 * pair : 2 * pair + 2, :, :],
                 in_=g_t[:].rearrange("p j u n -> p j n u"),
             )
-        g_codes = keep.tile([P, NT], U32, align_bytes=64)
-        g_scales = keep.tile([P, NT], U8, align_bytes=64)
-        nc.vector.quantize_mx(
-            out=g_codes[:].bitcast(E5M2_X4),
-            scales=g_scales[:],
-            in_=g_grouped[:].rearrange("p i n u -> p (i n u)").bitcast(BF16),
-        )
 
         iv_grouped = keep.tile([P, D, PACK], BF16, align_bytes=64)
         miv_grouped = keep.tile([P, D, PACK], BF16, align_bytes=64)
@@ -103,28 +106,33 @@ def tile_gaussianmlpbasislayer_pb_s_kernel(tc, xf, mean, var, grad_out, out):
         iv_scales = keep.tile([P, D], U8, align_bytes=64)
         miv_codes = keep.tile([P, D], U32, align_bytes=64)
         miv_scales = keep.tile([P, D], U8, align_bytes=64)
-        for c in range(COL_CHUNKS):
-            cols = slice(COL_CHUNK * c, COL_CHUNK * (c + 1))
-            nc.scalar.copy(out=by_word(iv_grouped, cols), in_=by_row(inv_var, cols))
-            nc.vector.tensor_tensor(
-                out=by_word(miv_grouped, cols), in0=by_row(mean_sb, cols), in1=by_row(inv_var, cols),
-                op=ALU.mult,
-            )
-        nc.vector.quantize_mx(
-            out=iv_codes[:].bitcast(E4M3_X4),
-            scales=iv_scales[:],
-            in_=iv_grouped[:].rearrange("p w t -> p (w t)"),
-        )
-        nc.vector.quantize_mx(
-            out=miv_codes[:].bitcast(E4M3_X4),
-            scales=miv_scales[:],
-            in_=miv_grouped[:].rearrange("p w t -> p (w t)"),
-        )
+        g_codes = keep.tile([P, NT], U32, align_bytes=64)
+        g_scales = keep.tile([P, NT], U8, align_bytes=64)
+        for step in range(COL_CHUNKS + LAG + 1):
+            if step < COL_CHUNKS:
+                nc.vector.tensor_copy(out=by_word(iv_grouped, step), in_=by_row(inv_var, step))
+            if step == COL_CHUNKS:
+                nc.vector.quantize_mx(
+                    out=g_codes[:].bitcast(E5M2_X4),
+                    scales=g_scales[:],
+                    in_=g_grouped[:].rearrange("p i n u -> p (i n u)").bitcast(BF16),
+                )
+            if 1 <= step <= COL_CHUNKS:
+                quantise_chunk(nc, iv_grouped, iv_codes, iv_scales, step - 1)
+            if LAG <= step < COL_CHUNKS + LAG:
+                nc.vector.tensor_tensor(
+                    out=by_word(miv_grouped, step - LAG),
+                    in0=by_row(mean_sb, step - LAG),
+                    in1=by_row(inv_var, step - LAG),
+                    op=ALU.mult,
+                )
+            if step >= LAG + 1:
+                quantise_chunk(nc, miv_grouped, miv_codes, miv_scales, step - LAG - 1)
 
         xf_b = []
         for i in range(ROW_TILES):
             rows = slice(P * i, P * (i + 1))
-            b_ps = psum_mm.tile([P, D], F32)
+            b_ps = psum.tile([P, D], F32, tag="bank")
             nc.tensor.matmul_mx(
                 out=b_ps[:],
                 lhsT=g_codes[:, rows].bitcast(E5M2_X4), lhsT_scale=g_scales[:, rows],
@@ -139,7 +147,7 @@ def tile_gaussianmlpbasislayer_pb_s_kernel(tc, xf, mean, var, grad_out, out):
         out_rows = out.rearrange("(p i) d -> p i d", i=ROW_TILES)
         for i in range(ROW_TILES):
             rows = slice(P * i, P * (i + 1))
-            a_ps = psum_mm.tile([P, D], F32)
+            a_ps = psum.tile([P, D], F32, tag="bank")
             nc.tensor.matmul_mx(
                 out=a_ps[:],
                 lhsT=g_codes[:, rows].bitcast(E5M2_X4), lhsT_scale=g_scales[:, rows],

@@ -76,6 +76,11 @@ def tile_gaussianmlpbasislayer_pb_s_kernel(tc, xf, mean, var, grad_out, out):
         identity = keep.tile([P, P], F32)
         masks.make_identity(nc, identity[:])
 
+        one = keep.tile([P, 1], F32)
+        nc.vector.memset(one[:], 1.0)
+        unused_root = keep.tile([P, 1], F32)
+        nc.scalar.activation(out=unused_root[:], in_=one[:], func=ACT.Abs_reciprocal_sqrt)
+
         rsqrt = keep.tile([P, PACK, D], F32)
         inv_var = keep.tile([P, PACK, D], F32)
         for step in range(COL_CHUNKS + 1):

@@ -18,22 +18,15 @@ K = P * PACK
 NT = 512
 D = 512
 ROW_TILES = NT // P
-HALF_K = K // 2
 PSUM_BANKS = 8
 COL_CHUNK = 64
 COL_CHUNKS = D // COL_CHUNK
 RUN = 4
 LAG = 2
+FIRST_COLS = 2 * COL_CHUNK
+LAST_PIECES = 2
 
 FLOPS = 2 * 2 * NT * K * D
-
-
-def load_k_rows(nc, rows_sb, rows):
-    for u in range(2):
-        nc.sync.dma_start(
-            out=rows_sb[:, 2 * u : 2 * u + 2, :],
-            in_=rows[HALF_K * u : HALF_K * (u + 1), :].rearrange("(p e) d -> p e d", e=2),
-        )
 
 
 def chunk_cols(c):
@@ -65,9 +58,11 @@ def tile_gaussianmlpbasislayer_pb_s_kernel(tc, xf, mean, var, grad_out, out):
         ctx.enter_context(tc.manual_schedule())
 
         var_sb = keep.tile([P, PACK, D], BF16)
-        load_k_rows(nc, var_sb, var)
+        var_rows = var.rearrange("(p t) d -> p t d", t=PACK)
+        nc.sync.dma_start(out=var_sb[:, :, :FIRST_COLS], in_=var_rows[:, :, :FIRST_COLS])
+        nc.sync.dma_start(out=var_sb[:, :, FIRST_COLS:], in_=var_rows[:, :, FIRST_COLS:])
         mean_sb = keep.tile([P, PACK, D], BF16)
-        load_k_rows(nc, mean_sb, mean)
+        nc.sync.dma_start(out=mean_sb[:], in_=mean.rearrange("(p t) d -> p t d", t=PACK))
         g_sb = keep.tile([P, ROW_TILES, K], BF16)
         nc.sync.dma_start(out=g_sb[:], in_=grad_out.rearrange("(p i) k -> p i k", i=ROW_TILES))
         xf_sb = keep.tile([P, ROW_TILES, D], BF16)
@@ -97,9 +92,9 @@ def tile_gaussianmlpbasislayer_pb_s_kernel(tc, xf, mean, var, grad_out, out):
         for pair in range(ROW_TILES // 2):
             g_t = psum.tile([P, 2, 2, P], F32, tag="bank")
             for j in range(2):
-                g_words = g_sb[:, 2 * pair + j, :].bitcast(F32)
+                g_words = g_sb[:, 2 * pair + j, :].bitcast(F32).rearrange("n (p u) -> n u p", u=2)
                 for u in range(2):
-                    nc.tensor.transpose(g_t[:, j, u, :], g_words[:, P * u : P * (u + 1)], identity[:])
+                    nc.tensor.transpose(g_t[:, j, u, :], g_words[:, u, :], identity[:])
             nc.scalar.copy(
                 out=g_grouped[:, 2 * pair : 2 * pair + 2, :, :],
                 in_=g_t[:].rearrange("p j u n -> p j n u"),
@@ -116,11 +111,15 @@ def tile_gaussianmlpbasislayer_pb_s_kernel(tc, xf, mean, var, grad_out, out):
         for step in range(COL_CHUNKS + LAG + 1):
             if step < COL_CHUNKS:
                 nc.vector.tensor_copy(out=by_word(iv_grouped, step), in_=by_row(inv_var, step))
-            if step == COL_CHUNKS:
+            if COL_CHUNKS <= step < COL_CHUNKS + ROW_TILES // 2:
+                pair = step - COL_CHUNKS
+                pair_rows = slice(2 * P * pair, 2 * P * (pair + 1))
                 nc.vector.quantize_mx(
-                    out=g_codes[:].bitcast(E5M2_X4),
-                    scales=g_scales[:],
-                    in_=g_grouped[:].rearrange("p i n u -> p (i n u)").bitcast(BF16),
+                    out=g_codes[:, pair_rows].bitcast(E5M2_X4),
+                    scales=g_scales[:, pair_rows],
+                    in_=g_grouped[:, 2 * pair : 2 * pair + 2, :, :]
+                    .rearrange("p j n u -> p (j n u)")
+                    .bitcast(BF16),
                 )
             if 1 <= step <= COL_CHUNKS:
                 quantise_chunk(nc, iv_grouped, iv_codes, iv_scales, step - 1)
@@ -159,5 +158,11 @@ def tile_gaussianmlpbasislayer_pb_s_kernel(tc, xf, mean, var, grad_out, out):
                 rhs=miv_codes[:].bitcast(E4M3_X4), rhs_scale=miv_scales[:],
                 start=True, stop=True,
             )
-            nc.vector.tensor_tensor(out=out_sb[:, i, :], in0=a_ps[:], in1=xf_b[i][:], op=ALU.subtract)
-            nc.sync.dma_start(out=out_rows[:, i, :], in_=out_sb[:, i, :])
+            pieces = LAST_PIECES if i == ROW_TILES - 1 else 1
+            width = D // pieces
+            for h in range(pieces):
+                cols = slice(width * h, width * (h + 1))
+                nc.vector.tensor_tensor(
+                    out=out_sb[:, i, cols], in0=a_ps[:, cols], in1=xf_b[i][:, cols], op=ALU.subtract
+                )
+                nc.sync.dma_start(out=out_rows[:, i, cols], in_=out_sb[:, i, cols])

@@ -22,9 +22,10 @@ PSUM_BANKS = 8
 COL_CHUNK = 64
 COL_CHUNKS = D // COL_CHUNK
 RUN = 4
-LAG = 2
+LAG = 1
 FIRST_COLS = 2 * COL_CHUNK
 LAST_PIECES = 2
+GPSIMD_TILE = 2
 
 FLOPS = 2 * 2 * NT * K * D
 
@@ -144,7 +145,12 @@ def tile_gaussianmlpbasislayer_pb_s_kernel(tc, xf, mean, var, grad_out, out):
                 start=True, stop=True,
             )
             product = products.tile([P, D], F32)
-            nc.vector.tensor_tensor(out=product[:], in0=b_ps[:], in1=xf_sb[:, i, :], op=ALU.mult)
+            if i == GPSIMD_TILE:
+                b_sb = keep.tile([P, D], F32)
+                nc.scalar.copy(out=b_sb[:], in_=b_ps[:])
+                nc.gpsimd.tensor_tensor(out=product[:], in0=b_sb[:], in1=xf_sb[:, i, :], op=ALU.mult)
+            else:
+                nc.vector.tensor_tensor(out=product[:], in0=b_ps[:], in1=xf_sb[:, i, :], op=ALU.mult)
             xf_b.append(product)
 
         out_sb = keep.tile([P, ROW_TILES, D], F32)

@@ -22,7 +22,7 @@ PSUM_BANKS = 8
 COL_CHUNK = 64
 COL_CHUNKS = D // COL_CHUNK
 RUN = 4
-LAG = 1
+LAG = 2
 FIRST_COLS = 2 * COL_CHUNK
 LAST_PIECES = 2
 GPSIMD_TILE = 2

@@ -25,6 +25,7 @@ RUN = 4
 LAG = 2
 FIRST_COLS = 2 * COL_CHUNK
 LAST_PIECES = 2
+WARM_UPS = 3
 GPSIMD_TILE = 2
 
 FLOPS = 2 * 2 * NT * K * D
@@ -133,6 +134,15 @@ def tile_gaussianmlpbasislayer_pb_s_kernel(tc, xf, mean, var, grad_out, out):
                 )
             if step >= LAG + 1:
                 quantise_chunk(nc, miv_grouped, miv_codes, miv_scales, step - LAG - 1)
+
+        unused_sums = psum.tile([P, D], F32, tag="bank")
+        iv_flat = iv_grouped[:].rearrange("p w t -> p (w t)")
+        for w in range(WARM_UPS):
+            first = D * (w + 1)
+            nc.tensor.matmul(
+                out=unused_sums[:], lhsT=iv_flat[:, first : first + P], rhs=iv_flat[:, first : first + D],
+                start=True, stop=True,
+            )
 
         xf_b = []
         for i in range(ROW_TILES):

@@ -144,41 +144,41 @@ def tile_gaussianmlpbasislayer_pb_s_kernel(tc, xf, mean, var, grad_out, out):
                 start=True, stop=True,
             )
 
-        xf_b = []
-        for i in range(ROW_TILES):
+        def mx_pass(i, codes, scales):
             rows = slice(P * i, P * (i + 1))
-            b_ps = psum.tile([P, D], F32, tag="bank")
+            sums = psum.tile([P, D], F32, tag="bank", name="sums")
             nc.tensor.matmul_mx(
-                out=b_ps[:],
+                out=sums[:],
                 lhsT=g_codes[:, rows].bitcast(E5M2_X4), lhsT_scale=g_scales[:, rows],
-                rhs=iv_codes[:].bitcast(E4M3_X4), rhs_scale=iv_scales[:],
+                rhs=codes[:].bitcast(E4M3_X4), rhs_scale=scales[:],
                 start=True, stop=True,
             )
-            product = products.tile([P, D], F32)
-            if i == GPSIMD_TILE:
-                b_sb = keep.tile([P, D], F32)
-                nc.scalar.copy(out=b_sb[:], in_=b_ps[:])
-                nc.gpsimd.tensor_tensor(out=product[:], in0=b_sb[:], in1=xf_sb[:, i, :], op=ALU.mult)
-            else:
-                nc.vector.tensor_tensor(out=product[:], in0=b_ps[:], in1=xf_sb[:, i, :], op=ALU.mult)
-            xf_b.append(product)
+            return sums
+
+        b_ps = [mx_pass(i, iv_codes, iv_scales) for i in range(ROW_TILES)]
+        xf_b = [products.tile([P, D], F32, name="product") for i in range(ROW_TILES)]
+        b_sb = keep.tile([P, D], F32)
+        nc.scalar.copy(out=b_sb[:], in_=b_ps[GPSIMD_TILE][:])
+        nc.gpsimd.tensor_tensor(
+            out=xf_b[GPSIMD_TILE][:], in0=b_sb[:], in1=xf_sb[:, GPSIMD_TILE, :], op=ALU.mult
+        )
+        a_ps = [mx_pass(i, miv_codes, miv_scales) for i in range(ROW_TILES)]
 
         out_sb = keep.tile([P, ROW_TILES, D], F32)
         out_rows = out.rearrange("(p i) d -> p i d", i=ROW_TILES)
+        def vector_product(i):
+            nc.vector.tensor_tensor(out=xf_b[i][:], in0=b_ps[i][:], in1=xf_sb[:, i, :], op=ALU.mult)
+
+        vector_tiles = [i for i in range(ROW_TILES) if i != GPSIMD_TILE]
+        vector_product(vector_tiles[0])
         for i in range(ROW_TILES):
-            rows = slice(P * i, P * (i + 1))
-            a_ps = psum.tile([P, D], F32, tag="bank")
-            nc.tensor.matmul_mx(
-                out=a_ps[:],
-                lhsT=g_codes[:, rows].bitcast(E5M2_X4), lhsT_scale=g_scales[:, rows],
-                rhs=miv_codes[:].bitcast(E4M3_X4), rhs_scale=miv_scales[:],
-                start=True, stop=True,
-            )
+            if i + 1 < len(vector_tiles):
+                vector_product(vector_tiles[i + 1])
             pieces = LAST_PIECES if i == ROW_TILES - 1 else 1
             width = D // pieces
             for h in range(pieces):
                 cols = slice(width * h, width * (h + 1))
                 nc.vector.tensor_tensor(
-                    out=out_sb[:, i, cols], in0=a_ps[:, cols], in1=xf_b[i][:, cols], op=ALU.subtract
+                    out=out_sb[:, i, cols], in0=a_ps[i][:, cols], in1=xf_b[i][:, cols], op=ALU.subtract
                 )
                 nc.sync.dma_start(out=out_rows[:, i, cols], in_=out_sb[:, i, cols])

@@ -22,11 +22,12 @@ PSUM_BANKS = 8
 COL_CHUNK = 64
 COL_CHUNKS = D // COL_CHUNK
 RUN = 4
-LAG = 2
-FIRST_COLS = 2 * COL_CHUNK
+VAR_FIRST_COLS = 128
+MEAN_FIRST_COLS = 256
 LAST_PIECES = 2
+GPSIMD_TILES = (2,)
+PAIR_ORDER = (0, 1)
 WARM_UPS = 3
-GPSIMD_TILE = 2
 
 FLOPS = 2 * 2 * NT * K * D
 
@@ -56,18 +57,21 @@ def tile_gaussianmlpbasislayer_pb_s_kernel(tc, xf, mean, var, grad_out, out):
     with ExitStack() as ctx:
         keep = ctx.enter_context(tc.tile_pool(name="keep", bufs=1))
         products = ctx.enter_context(tc.tile_pool(name="products", bufs=ROW_TILES))
+        copies = ctx.enter_context(tc.tile_pool(name="copies", bufs=len(GPSIMD_TILES)))
         psum = ctx.enter_context(tc.psum_pool(name="psum", bufs=PSUM_BANKS))
         ctx.enter_context(tc.manual_schedule())
 
         var_sb = keep.tile([P, PACK, D], BF16)
         var_rows = var.rearrange("(p t) d -> p t d", t=PACK)
-        nc.sync.dma_start(out=var_sb[:, :, :FIRST_COLS], in_=var_rows[:, :, :FIRST_COLS])
-        nc.sync.dma_start(out=var_sb[:, :, FIRST_COLS:], in_=var_rows[:, :, FIRST_COLS:])
         mean_sb = keep.tile([P, PACK, D], BF16)
-        nc.sync.dma_start(out=mean_sb[:], in_=mean.rearrange("(p t) d -> p t d", t=PACK))
+        mean_rows = mean.rearrange("(p t) d -> p t d", t=PACK)
         g_sb = keep.tile([P, ROW_TILES, K], BF16)
-        nc.sync.dma_start(out=g_sb[:], in_=grad_out.rearrange("(p i) k -> p i k", i=ROW_TILES))
         xf_sb = keep.tile([P, ROW_TILES, D], BF16)
+        nc.sync.dma_start(out=var_sb[:, :, :VAR_FIRST_COLS], in_=var_rows[:, :, :VAR_FIRST_COLS])
+        nc.sync.dma_start(out=var_sb[:, :, VAR_FIRST_COLS:], in_=var_rows[:, :, VAR_FIRST_COLS:])
+        nc.sync.dma_start(out=mean_sb[:, :, :MEAN_FIRST_COLS], in_=mean_rows[:, :, :MEAN_FIRST_COLS])
+        nc.sync.dma_start(out=g_sb[:], in_=grad_out.rearrange("(p i) k -> p i k", i=ROW_TILES))
+        nc.sync.dma_start(out=mean_sb[:, :, MEAN_FIRST_COLS:], in_=mean_rows[:, :, MEAN_FIRST_COLS:])
         nc.sync.dma_start(out=xf_sb[:], in_=xf.rearrange("(p i) d -> p i d", i=ROW_TILES))
 
         identity = keep.tile([P, P], F32)
@@ -78,29 +82,36 @@ def tile_gaussianmlpbasislayer_pb_s_kernel(tc, xf, mean, var, grad_out, out):
         unused_root = keep.tile([P, 1], F32)
         nc.scalar.activation(out=unused_root[:], in_=one[:], func=ACT.Abs_reciprocal_sqrt)
 
+        g_t = {}
+        for pair in PAIR_ORDER:
+            g_t[pair] = psum.tile([P, 2, 2, P], F32, tag="bank", name="g_t")
+            for j in range(2):
+                g_words = g_sb[:, 2 * pair + j, :].bitcast(F32).rearrange("n (p u) -> n u p", u=2)
+                for u in range(2):
+                    nc.tensor.transpose(g_t[pair][:, j, u, :], g_words[:, u, :], identity[:])
+
         rsqrt = keep.tile([P, PACK, D], F32)
         inv_var = keep.tile([P, PACK, D], F32)
+        g_grouped = keep.tile([P, ROW_TILES, P, 2], F32, align_bytes=64)
+
+        def copy_pair(pair):
+            nc.scalar.copy(
+                out=g_grouped[:, 2 * pair : 2 * pair + 2, :, :],
+                in_=g_t[pair][:].rearrange("p j u n -> p j n u"),
+            )
+
         for step in range(COL_CHUNKS + 1):
             if step < COL_CHUNKS:
                 cols = chunk_cols(step)
                 nc.scalar.activation(
                     out=rsqrt[:, :, cols], in_=var_sb[:, :, cols], func=ACT.Abs_reciprocal_sqrt
                 )
+            if step == COL_CHUNKS:
+                copy_pair(PAIR_ORDER[0])
             if step >= 1:
                 cols = chunk_cols(step - 1)
                 nc.scalar.activation(out=inv_var[:, :, cols], in_=rsqrt[:, :, cols], func=ACT.Square)
-
-        g_grouped = keep.tile([P, ROW_TILES, P, 2], F32, align_bytes=64)
-        for pair in range(ROW_TILES // 2):
-            g_t = psum.tile([P, 2, 2, P], F32, tag="bank")
-            for j in range(2):
-                g_words = g_sb[:, 2 * pair + j, :].bitcast(F32).rearrange("n (p u) -> n u p", u=2)
-                for u in range(2):
-                    nc.tensor.transpose(g_t[:, j, u, :], g_words[:, u, :], identity[:])
-            nc.scalar.copy(
-                out=g_grouped[:, 2 * pair : 2 * pair + 2, :, :],
-                in_=g_t[:].rearrange("p j u n -> p j n u"),
-            )
+        copy_pair(PAIR_ORDER[1])
 
         iv_grouped = keep.tile([P, D, PACK], BF16, align_bytes=64)
         miv_grouped = keep.tile([P, D, PACK], BF16, align_bytes=64)
@@ -110,30 +121,39 @@ def tile_gaussianmlpbasislayer_pb_s_kernel(tc, xf, mean, var, grad_out, out):
         miv_scales = keep.tile([P, D], U8, align_bytes=64)
         g_codes = keep.tile([P, NT], U32, align_bytes=64)
         g_scales = keep.tile([P, NT], U8, align_bytes=64)
-        for step in range(COL_CHUNKS + LAG + 1):
+
+        def quantise_pair(pair):
+            pair_rows = slice(2 * P * pair, 2 * P * (pair + 1))
+            nc.vector.quantize_mx(
+                out=g_codes[:, pair_rows].bitcast(E5M2_X4),
+                scales=g_scales[:, pair_rows],
+                in_=g_grouped[:, 2 * pair : 2 * pair + 2, :, :]
+                .rearrange("p j n u -> p (j n u)")
+                .bitcast(BF16),
+            )
+
+        def mean_times_inv_var(c):
+            nc.vector.tensor_tensor(
+                out=by_word(miv_grouped, c), in0=by_row(mean_sb, c), in1=by_row(inv_var, c), op=ALU.mult
+            )
+            if c >= 1:
+                quantise_chunk(nc, miv_grouped, miv_codes, miv_scales, c - 1)
+
+        made = 0
+        for step in range(COL_CHUNKS + 1):
             if step < COL_CHUNKS:
                 nc.vector.tensor_copy(out=by_word(iv_grouped, step), in_=by_row(inv_var, step))
-            if COL_CHUNKS <= step < COL_CHUNKS + ROW_TILES // 2:
-                pair = step - COL_CHUNKS
-                pair_rows = slice(2 * P * pair, 2 * P * (pair + 1))
-                nc.vector.quantize_mx(
-                    out=g_codes[:, pair_rows].bitcast(E5M2_X4),
-                    scales=g_scales[:, pair_rows],
-                    in_=g_grouped[:, 2 * pair : 2 * pair + 2, :, :]
-                    .rearrange("p j n u -> p (j n u)")
-                    .bitcast(BF16),
-                )
-            if 1 <= step <= COL_CHUNKS:
+            if step == COL_CHUNKS:
+                quantise_pair(PAIR_ORDER[0])
+            if step >= 1:
                 quantise_chunk(nc, iv_grouped, iv_codes, iv_scales, step - 1)
-            if LAG <= step < COL_CHUNKS + LAG:
-                nc.vector.tensor_tensor(
-                    out=by_word(miv_grouped, step - LAG),
-                    in0=by_row(mean_sb, step - LAG),
-                    in1=by_row(inv_var, step - LAG),
-                    op=ALU.mult,
-                )
-            if step >= LAG + 1:
-                quantise_chunk(nc, miv_grouped, miv_codes, miv_scales, step - LAG - 1)
+            if 1 <= step:
+                mean_times_inv_var(made)
+                made += 1
+        quantise_pair(PAIR_ORDER[1])
+        for c in range(made, COL_CHUNKS):
+            mean_times_inv_var(c)
+        quantise_chunk(nc, miv_grouped, miv_codes, miv_scales, COL_CHUNKS - 1)
 
         unused_sums = psum.tile([P, D], F32, tag="bank")
         iv_flat = iv_grouped[:].rearrange("p w t -> p (w t)")
@@ -155,21 +175,25 @@ def tile_gaussianmlpbasislayer_pb_s_kernel(tc, xf, mean, var, grad_out, out):
             )
             return sums
 
-        b_ps = [mx_pass(i, iv_codes, iv_scales) for i in range(ROW_TILES)]
-        xf_b = [products.tile([P, D], F32, name="product") for i in range(ROW_TILES)]
-        b_sb = keep.tile([P, D], F32)
-        nc.scalar.copy(out=b_sb[:], in_=b_ps[GPSIMD_TILE][:])
-        nc.gpsimd.tensor_tensor(
-            out=xf_b[GPSIMD_TILE][:], in0=b_sb[:], in1=xf_sb[:, GPSIMD_TILE, :], op=ALU.mult
-        )
+        tile_order = [2 * pair + j for pair in PAIR_ORDER for j in range(2)]
+        b_ps = {}
+        xf_b = {}
+        for i in tile_order:
+            b_ps[i] = mx_pass(i, iv_codes, iv_scales)
+            xf_b[i] = products.tile([P, D], F32, name="product")
+        for i in GPSIMD_TILES:
+            b_sb = copies.tile([P, D], F32, name="b_sb")
+            nc.scalar.copy(out=b_sb[:], in_=b_ps[i][:])
+            nc.gpsimd.tensor_tensor(out=xf_b[i][:], in0=b_sb[:], in1=xf_sb[:, i, :], op=ALU.mult)
         a_ps = [mx_pass(i, miv_codes, miv_scales) for i in range(ROW_TILES)]
 
         out_sb = keep.tile([P, ROW_TILES, D], F32)
         out_rows = out.rearrange("(p i) d -> p i d", i=ROW_TILES)
+
         def vector_product(i):
             nc.vector.tensor_tensor(out=xf_b[i][:], in0=b_ps[i][:], in1=xf_sb[:, i, :], op=ALU.mult)
 
-        vector_tiles = [i for i in range(ROW_TILES) if i != GPSIMD_TILE]
+        vector_tiles = [i for i in range(ROW_TILES) if i not in GPSIMD_TILES]
         vector_product(vector_tiles[0])
         for i in range(ROW_TILES):
             if i + 1 < len(vector_tiles):

@@ -25,8 +25,8 @@ RUN = 4
 VAR_FIRST_COLS = 128
 MEAN_FIRST_COLS = 256
 LAST_PIECES = 2
-GPSIMD_TILES = (2,)
-PAIR_ORDER = (0, 1)
+GPSIMD_TILES = (2, 3)
+PAIR_ORDER = (1, 0)
 WARM_UPS = 3
 
 FLOPS = 2 * 2 * NT * K * D
@@ -147,10 +147,11 @@ def tile_gaussianmlpbasislayer_pb_s_kernel(tc, xf, mean, var, grad_out, out):
                 quantise_pair(PAIR_ORDER[0])
             if step >= 1:
                 quantise_chunk(nc, iv_grouped, iv_codes, iv_scales, step - 1)
+            if step == COL_CHUNKS:
+                quantise_pair(PAIR_ORDER[1])
             if 1 <= step:
                 mean_times_inv_var(made)
                 made += 1
-        quantise_pair(PAIR_ORDER[1])
         for c in range(made, COL_CHUNKS):
             mean_times_inv_var(c)
         quantise_chunk(nc, miv_grouped, miv_codes, miv_scales, COL_CHUNKS - 1)
@@ -175,12 +176,13 @@ def tile_gaussianmlpbasislayer_pb_s_kernel(tc, xf, mean, var, grad_out, out):
             )
             return sums
 
-        tile_order = [2 * pair + j for pair in PAIR_ORDER for j in range(2)]
+        tile_order = (2, 0, 3, 1)
         b_ps = {}
         xf_b = {}
         for i in tile_order:
             b_ps[i] = mx_pass(i, iv_codes, iv_scales)
             xf_b[i] = products.tile([P, D], F32, name="product")
+        nc.vector.memset(xf_b[GPSIMD_TILES[0]][:, :1], 0.0)
         for i in GPSIMD_TILES:
             b_sb = copies.tile([P, D], F32, name="b_sb")
             nc.scalar.copy(out=b_sb[:], in_=b_ps[i][:])

@@ -25,8 +25,8 @@ RUN = 4
 VAR_FIRST_COLS = 128
 MEAN_FIRST_COLS = 256
 LAST_PIECES = 2
-GPSIMD_TILES = (2, 3)
-PAIR_ORDER = (1, 0)
+GPSIMD_TILES = (0, 2)
+PAIR_ORDER = (0, 1)
 WARM_UPS = 3
 
 FLOPS = 2 * 2 * NT * K * D
@@ -106,12 +106,11 @@ def tile_gaussianmlpbasislayer_pb_s_kernel(tc, xf, mean, var, grad_out, out):
                 nc.scalar.activation(
                     out=rsqrt[:, :, cols], in_=var_sb[:, :, cols], func=ACT.Abs_reciprocal_sqrt
                 )
-            if step == COL_CHUNKS:
-                copy_pair(PAIR_ORDER[0])
             if step >= 1:
                 cols = chunk_cols(step - 1)
                 nc.scalar.activation(out=inv_var[:, :, cols], in_=rsqrt[:, :, cols], func=ACT.Square)
-        copy_pair(PAIR_ORDER[1])
+        for pair in PAIR_ORDER:
+            copy_pair(pair)
 
         iv_grouped = keep.tile([P, D, PACK], BF16, align_bytes=64)
         miv_grouped = keep.tile([P, D, PACK], BF16, align_bytes=64)
@@ -132,29 +131,30 @@ def tile_gaussianmlpbasislayer_pb_s_kernel(tc, xf, mean, var, grad_out, out):
                 .bitcast(BF16),
             )
 
+        def round_inv_var(c):
+            nc.vector.tensor_copy(out=by_word(iv_grouped, c), in_=by_row(inv_var, c))
+
         def mean_times_inv_var(c):
             nc.vector.tensor_tensor(
                 out=by_word(miv_grouped, c), in0=by_row(mean_sb, c), in1=by_row(inv_var, c), op=ALU.mult
             )
+
+        last = COL_CHUNKS - 1
+        for c in range(last):
+            round_inv_var(c)
+            if c >= 1:
+                quantise_chunk(nc, iv_grouped, iv_codes, iv_scales, c - 1)
+            mean_times_inv_var(c)
             if c >= 1:
                 quantise_chunk(nc, miv_grouped, miv_codes, miv_scales, c - 1)
-
-        made = 0
-        for step in range(COL_CHUNKS + 1):
-            if step < COL_CHUNKS:
-                nc.vector.tensor_copy(out=by_word(iv_grouped, step), in_=by_row(inv_var, step))
-            if step == COL_CHUNKS:
-                quantise_pair(PAIR_ORDER[0])
-            if step >= 1:
-                quantise_chunk(nc, iv_grouped, iv_codes, iv_scales, step - 1)
-            if step == COL_CHUNKS:
-                quantise_pair(PAIR_ORDER[1])
-            if 1 <= step:
-                mean_times_inv_var(made)
-                made += 1
-        for c in range(made, COL_CHUNKS):
-            mean_times_inv_var(c)
-        quantise_chunk(nc, miv_grouped, miv_codes, miv_scales, COL_CHUNKS - 1)
+        round_inv_var(last)
+        quantise_chunk(nc, iv_grouped, iv_codes, iv_scales, last - 1)
+        quantise_pair(PAIR_ORDER[0])
+        quantise_chunk(nc, iv_grouped, iv_codes, iv_scales, last)
+        mean_times_inv_var(last)
+        quantise_chunk(nc, miv_grouped, miv_codes, miv_scales, last - 1)
+        quantise_pair(PAIR_ORDER[1])
+        quantise_chunk(nc, miv_grouped, miv_codes, miv_scales, last)
 
         unused_sums = psum.tile([P, D], F32, tag="bank")
         iv_flat = iv_grouped[:].rearrange("p w t -> p (w t)")
@@ -176,7 +176,7 @@ def tile_gaussianmlpbasislayer_pb_s_kernel(tc, xf, mean, var, grad_out, out):
             )
             return sums
 
-        tile_order = (2, 0, 3, 1)
+        tile_order = [2 * pair + j for pair in PAIR_ORDER for j in range(2)]
         b_ps = {}
         xf_b = {}
         for i in tile_order:
@@ -187,7 +187,11 @@ def tile_gaussianmlpbasislayer_pb_s_kernel(tc, xf, mean, var, grad_out, out):
             b_sb = copies.tile([P, D], F32, name="b_sb")
             nc.scalar.copy(out=b_sb[:], in_=b_ps[i][:])
             nc.gpsimd.tensor_tensor(out=xf_b[i][:], in0=b_sb[:], in1=xf_sb[:, i, :], op=ALU.mult)
-        a_ps = [mx_pass(i, miv_codes, miv_scales) for i in range(ROW_TILES)]
+        vector_tiles = [i for i in range(ROW_TILES) if i not in GPSIMD_TILES]
+        end_order = vector_tiles + list(GPSIMD_TILES)
+        a_ps = {}
+        for i in end_order:
+            a_ps[i] = mx_pass(i, miv_codes, miv_scales)
 
         out_sb = keep.tile([P, ROW_TILES, D], F32)
         out_rows = out.rearrange("(p i) d -> p i d", i=ROW_TILES)
@@ -195,12 +199,10 @@ def tile_gaussianmlpbasislayer_pb_s_kernel(tc, xf, mean, var, grad_out, out):
         def vector_product(i):
             nc.vector.tensor_tensor(out=xf_b[i][:], in0=b_ps[i][:], in1=xf_sb[:, i, :], op=ALU.mult)
 
-        vector_tiles = [i for i in range(ROW_TILES) if i not in GPSIMD_TILES]
-        vector_product(vector_tiles[0])
-        for i in range(ROW_TILES):
-            if i + 1 < len(vector_tiles):
-                vector_product(vector_tiles[i + 1])
-            pieces = LAST_PIECES if i == ROW_TILES - 1 else 1
+        for i in vector_tiles:
+            vector_product(i)
+        for i in end_order:
+            pieces = LAST_PIECES if i == end_order[-1] else 1
             width = D // pieces
             for h in range(pieces):
                 cols = slice(width * h, width * (h + 1))

@@ -22,8 +22,7 @@ PSUM_BANKS = 8
 COL_CHUNK = 64
 COL_CHUNKS = D // COL_CHUNK
 RUN = 4
-VAR_FIRST_COLS = 128
-MEAN_FIRST_COLS = 256
+FIRST_COLS = 256
 LAST_PIECES = 2
 GPSIMD_TILES = (0, 2)
 PAIR_ORDER = (0, 1)
@@ -67,11 +66,14 @@ def tile_gaussianmlpbasislayer_pb_s_kernel(tc, xf, mean, var, grad_out, out):
         mean_rows = mean.rearrange("(p t) d -> p t d", t=PACK)
         g_sb = keep.tile([P, ROW_TILES, K], BF16)
         xf_sb = keep.tile([P, ROW_TILES, D], BF16)
-        nc.sync.dma_start(out=var_sb[:, :, :VAR_FIRST_COLS], in_=var_rows[:, :, :VAR_FIRST_COLS])
-        nc.sync.dma_start(out=var_sb[:, :, VAR_FIRST_COLS:], in_=var_rows[:, :, VAR_FIRST_COLS:])
-        nc.sync.dma_start(out=mean_sb[:, :, :MEAN_FIRST_COLS], in_=mean_rows[:, :, :MEAN_FIRST_COLS])
-        nc.sync.dma_start(out=g_sb[:], in_=grad_out.rearrange("(p i) k -> p i k", i=ROW_TILES))
-        nc.sync.dma_start(out=mean_sb[:, :, MEAN_FIRST_COLS:], in_=mean_rows[:, :, MEAN_FIRST_COLS:])
+        g_rows = grad_out.rearrange("(p i) k -> p i k", i=ROW_TILES)
+        first, rest = slice(0, FIRST_COLS), slice(FIRST_COLS, D)
+        nc.sync.dma_start(out=var_sb[:, :, first], in_=var_rows[:, :, first])
+        nc.sync.dma_start(out=mean_sb[:, :, first], in_=mean_rows[:, :, first])
+        nc.sync.dma_start(out=var_sb[:, :, rest], in_=var_rows[:, :, rest])
+        nc.sync.dma_start(out=g_sb[:, 0:2, :], in_=g_rows[:, 0:2, :])
+        nc.sync.dma_start(out=mean_sb[:, :, rest], in_=mean_rows[:, :, rest])
+        nc.sync.dma_start(out=g_sb[:, 2:4, :], in_=g_rows[:, 2:4, :])
         nc.sync.dma_start(out=xf_sb[:], in_=xf.rearrange("(p i) d -> p i d", i=ROW_TILES))
 
         identity = keep.tile([P, P], F32)

@@ -26,7 +26,7 @@ FIRST_COLS = 256
 LAST_PIECES = 2
 GPSIMD_TILES = (0, 2)
 PAIR_ORDER = (0, 1)
-WARM_UPS = 3
+WARM_COLS = 2 * COL_CHUNK
 
 FLOPS = 2 * 2 * NT * K * D
 
@@ -84,14 +84,6 @@ def tile_gaussianmlpbasislayer_pb_s_kernel(tc, xf, mean, var, grad_out, out):
         unused_root = keep.tile([P, 1], F32)
         nc.scalar.activation(out=unused_root[:], in_=one[:], func=ACT.Abs_reciprocal_sqrt)
 
-        g_t = {}
-        for pair in PAIR_ORDER:
-            g_t[pair] = psum.tile([P, 2, 2, P], F32, tag="bank", name="g_t")
-            for j in range(2):
-                g_words = g_sb[:, 2 * pair + j, :].bitcast(F32).rearrange("n (p u) -> n u p", u=2)
-                for u in range(2):
-                    nc.tensor.transpose(g_t[pair][:, j, u, :], g_words[:, u, :], identity[:])
-
         rsqrt = keep.tile([P, PACK, D], F32)
         inv_var = keep.tile([P, PACK, D], F32)
         g_grouped = keep.tile([P, ROW_TILES, P, 2], F32, align_bytes=64)
@@ -111,6 +103,36 @@ def tile_gaussianmlpbasislayer_pb_s_kernel(tc, xf, mean, var, grad_out, out):
             if step >= 1:
                 cols = chunk_cols(step - 1)
                 nc.scalar.activation(out=inv_var[:, :, cols], in_=rsqrt[:, :, cols], func=ACT.Square)
+
+        g_t = {}
+        for pair in PAIR_ORDER:
+            g_t[pair] = psum.tile([P, 2, 2, P], F32, tag="bank", name="g_t")
+        unused_sums = psum.tile([P, WARM_COLS], F32, tag="bank")
+
+        def transpose_pair(pair):
+            for j in range(2):
+                g_words = g_sb[:, 2 * pair + j, :].bitcast(F32).rearrange("n (p u) -> n u p", u=2)
+                for u in range(2):
+                    nc.tensor.transpose(g_t[pair][:, j, u, :], g_words[:, u, :], identity[:])
+
+        def warm_up(values, c):
+            first = COL_CHUNK * (c - 1)
+            nc.tensor.matmul(
+                out=unused_sums[:], lhsT=identity[:], rhs=values[:, 0, first : first + WARM_COLS],
+                start=True, stop=True,
+            )
+
+        for c in (1, 2, 3):
+            warm_up(rsqrt, c)
+        transpose_pair(PAIR_ORDER[0])
+        for c in (4, 5):
+            warm_up(rsqrt, c)
+        transpose_pair(PAIR_ORDER[1])
+        for c in (6, 7):
+            warm_up(rsqrt, c)
+        for c in (6, 7):
+            warm_up(inv_var, c)
+
         for pair in PAIR_ORDER:
             copy_pair(pair)
 
@@ -157,15 +179,6 @@ def tile_gaussianmlpbasislayer_pb_s_kernel(tc, xf, mean, var, grad_out, out):
         quantise_chunk(nc, miv_grouped, miv_codes, miv_scales, last - 1)
         quantise_pair(PAIR_ORDER[1])
         quantise_chunk(nc, miv_grouped, miv_codes, miv_scales, last)
-
-        unused_sums = psum.tile([P, D], F32, tag="bank")
-        iv_flat = iv_grouped[:].rearrange("p w t -> p (w t)")
-        for w in range(WARM_UPS):
-            first = D * (w + 1)
-            nc.tensor.matmul(
-                out=unused_sums[:], lhsT=iv_flat[:, first : first + P], rhs=iv_flat[:, first : first + D],
-                start=True, stop=True,
-            )
 
         def mx_pass(i, codes, scales):
             rows = slice(P * i, P * (i + 1))

@@ -212,7 +212,7 @@ def tile_gaussianmlpbasislayer_pb_s_kernel(tc, xf, mean, var, grad_out, out):
         out_rows = out.rearrange("(p i) d -> p i d", i=ROW_TILES)
 
         def vector_product(i):
-            nc.vector.tensor_tensor(out=xf_b[i][:], in0=b_ps[i][:], in1=xf_sb[:, i, :], op=ALU.mult)
+            nc.vector.tensor_tensor(out=xf_b[i][:], in0=xf_sb[:, i, :], in1=b_ps[i][:], op=ALU.mult)
 
         for i in vector_tiles:
             vector_product(i)
@@ -221,7 +221,8 @@ def tile_gaussianmlpbasislayer_pb_s_kernel(tc, xf, mean, var, grad_out, out):
             width = D // pieces
             for h in range(pieces):
                 cols = slice(width * h, width * (h + 1))
-                nc.vector.tensor_tensor(
-                    out=out_sb[:, i, cols], in0=a_ps[i][:, cols], in1=xf_b[i][:, cols], op=ALU.subtract
+                nc.vector.scalar_tensor_tensor(
+                    out=out_sb[:, i, cols], in0=xf_b[i][:, cols], scalar=-1.0, in1=a_ps[i][:, cols],
+                    op0=ALU.mult, op1=ALU.add,
                 )
                 nc.sync.dma_start(out=out_rows[:, i, cols], in_=out_sb[:, i, cols])

@@ -35,12 +35,16 @@ def chunk_cols(c):
     return slice(COL_CHUNK * c, COL_CHUNK * (c + 1))
 
 
-def by_row(plane_major, c):
-    return plane_major[:, :, chunk_cols(c)].rearrange("p t (g i) -> p g t i", i=RUN)
+def half_cols(h):
+    return slice(COL_CHUNK // 2 * h, COL_CHUNK // 2 * (h + 1))
 
 
-def by_word(grouped, c):
-    return grouped[:, chunk_cols(c), :].rearrange("p (g i) t -> p g t i", i=RUN)
+def by_row(plane_major, cols):
+    return plane_major[:, :, cols].rearrange("p t (g i) -> p g t i", i=RUN)
+
+
+def by_word(grouped, cols):
+    return grouped[:, cols, :].rearrange("p (g i) t -> p g t i", i=RUN)
 
 
 def quantise_chunk(nc, grouped, codes, scales, c):
@@ -94,15 +98,17 @@ def tile_gaussianmlpbasislayer_pb_s_kernel(tc, xf, mean, var, grad_out, out):
                 in_=g_t[pair][:].rearrange("p j u n -> p j n u"),
             )
 
-        for step in range(COL_CHUNKS + 1):
-            if step < COL_CHUNKS:
-                cols = chunk_cols(step)
-                nc.scalar.activation(
-                    out=rsqrt[:, :, cols], in_=var_sb[:, :, cols], func=ACT.Abs_reciprocal_sqrt
-                )
-            if step >= 1:
-                cols = chunk_cols(step - 1)
-                nc.scalar.activation(out=inv_var[:, :, cols], in_=rsqrt[:, :, cols], func=ACT.Square)
+        def root(cols):
+            nc.scalar.activation(out=rsqrt[:, :, cols], in_=var_sb[:, :, cols], func=ACT.Abs_reciprocal_sqrt)
+
+        root(half_cols(0))
+        root(half_cols(1))
+        root(chunk_cols(1))
+        for c in range(1, COL_CHUNKS):
+            if c + 1 < COL_CHUNKS:
+                root(chunk_cols(c + 1))
+            cols = chunk_cols(c)
+            nc.scalar.activation(out=inv_var[:, :, cols], in_=rsqrt[:, :, cols], func=ACT.Square)
 
         g_t = {}
         for pair in PAIR_ORDER:
@@ -155,27 +161,34 @@ def tile_gaussianmlpbasislayer_pb_s_kernel(tc, xf, mean, var, grad_out, out):
                 .bitcast(BF16),
             )
 
-        def round_inv_var(c):
-            nc.vector.tensor_copy(out=by_word(iv_grouped, c), in_=by_row(inv_var, c))
+        def round_inv_var(cols):
+            nc.vector.tensor_copy(out=by_word(iv_grouped, cols), in_=by_row(inv_var, cols))
 
-        def mean_times_inv_var(c):
+        def mean_times_inv_var(cols):
             nc.vector.tensor_tensor(
-                out=by_word(miv_grouped, c), in0=by_row(mean_sb, c), in1=by_row(inv_var, c), op=ALU.mult
+                out=by_word(miv_grouped, cols), in0=by_row(mean_sb, cols), in1=by_row(inv_var, cols), op=ALU.mult
             )
 
         last = COL_CHUNKS - 1
-        for c in range(last):
-            round_inv_var(c)
-            if c >= 1:
-                quantise_chunk(nc, iv_grouped, iv_codes, iv_scales, c - 1)
-            mean_times_inv_var(c)
-            if c >= 1:
-                quantise_chunk(nc, miv_grouped, miv_codes, miv_scales, c - 1)
-        round_inv_var(last)
+        for h in range(2):
+            cols = half_cols(h)
+            nc.vector.tensor_tensor(
+                out=inv_var[:, :, cols], in0=rsqrt[:, :, cols], in1=rsqrt[:, :, cols], op=ALU.mult
+            )
+        for h in range(2):
+            round_inv_var(half_cols(h))
+        for h in range(2):
+            mean_times_inv_var(half_cols(h))
+        for c in range(1, last):
+            round_inv_var(chunk_cols(c))
+            quantise_chunk(nc, iv_grouped, iv_codes, iv_scales, c - 1)
+            mean_times_inv_var(chunk_cols(c))
+            quantise_chunk(nc, miv_grouped, miv_codes, miv_scales, c - 1)
+        round_inv_var(chunk_cols(last))
         quantise_chunk(nc, iv_grouped, iv_codes, iv_scales, last - 1)
         quantise_pair(PAIR_ORDER[0])
         quantise_chunk(nc, iv_grouped, iv_codes, iv_scales, last)
-        mean_times_inv_var(last)
+        mean_times_inv_var(chunk_cols(last))
         quantise_chunk(nc, miv_grouped, miv_codes, miv_scales, last - 1)
         quantise_pair(PAIR_ORDER[1])
         quantise_chunk(nc, miv_grouped, miv_codes, miv_scales, last)

from contextlib import ExitStack

import concourse.masks as masks
import concourse.mybir as mybir

F32 = mybir.dt.float32
BF16 = mybir.dt.bfloat16
U32 = mybir.dt.uint32
U8 = mybir.dt.uint8
E4M3_X4 = mybir.dt.float8_e4m3fn_x4
E5M2_X4 = mybir.dt.float8_e5m2_x4
ACT = mybir.ActivationFunctionType
ALU = mybir.AluOpType

P = 128
PACK = 4
K = P * PACK
NT = 512
D = 512
ROW_TILES = NT // P
PSUM_BANKS = 8
COL_CHUNK = 64
COL_CHUNKS = D // COL_CHUNK
RUN = 4
FIRST_COLS = 256
LAST_PIECES = 2
GPSIMD_TILES = (0, 2)
PAIR_ORDER = (0, 1)
WARM_COLS = 2 * COL_CHUNK

FLOPS = 2 * 2 * NT * K * D


def chunk_cols(c):
    return slice(COL_CHUNK * c, COL_CHUNK * (c + 1))


def half_cols(h):
    return slice(COL_CHUNK // 2 * h, COL_CHUNK // 2 * (h + 1))


def by_row(plane_major, cols):
    return plane_major[:, :, cols].rearrange("p t (g i) -> p g t i", i=RUN)


def by_word(grouped, cols):
    return grouped[:, cols, :].rearrange("p (g i) t -> p g t i", i=RUN)


def quantise_chunk(nc, grouped, codes, scales, c):
    nc.vector.quantize_mx(
        out=codes[:, chunk_cols(c)].bitcast(E4M3_X4),
        scales=scales[:, chunk_cols(c)],
        in_=grouped[:, chunk_cols(c), :].rearrange("p w t -> p (w t)"),
    )


def tile_gaussianmlpbasislayer_pb_s_kernel(tc, xf, mean, var, grad_out, out):
    nc = tc.nc
    with ExitStack() as ctx:
        keep = ctx.enter_context(tc.tile_pool(name="keep", bufs=1))
        products = ctx.enter_context(tc.tile_pool(name="products", bufs=ROW_TILES))
        copies = ctx.enter_context(tc.tile_pool(name="copies", bufs=len(GPSIMD_TILES)))
        psum = ctx.enter_context(tc.psum_pool(name="psum", bufs=PSUM_BANKS))
        ctx.enter_context(tc.manual_schedule())

        var_sb = keep.tile([P, PACK, D], BF16)
        var_rows = var.rearrange("(p t) d -> p t d", t=PACK)
        mean_sb = keep.tile([P, PACK, D], BF16)
        mean_rows = mean.rearrange("(p t) d -> p t d", t=PACK)
        g_sb = keep.tile([P, ROW_TILES, K], BF16)
        xf_sb = keep.tile([P, ROW_TILES, D], BF16)
        g_rows = grad_out.rearrange("(p i) k -> p i k", i=ROW_TILES)
        first, rest = slice(0, FIRST_COLS), slice(FIRST_COLS, D)
        nc.sync.dma_start(out=var_sb[:, :, first], in_=var_rows[:, :, first])
        nc.sync.dma_start(out=mean_sb[:, :, first], in_=mean_rows[:, :, first])
        nc.sync.dma_start(out=var_sb[:, :, rest], in_=var_rows[:, :, rest])
        nc.sync.dma_start(out=g_sb[:, 0:2, :], in_=g_rows[:, 0:2, :])
        nc.sync.dma_start(out=mean_sb[:, :, rest], in_=mean_rows[:, :, rest])
        nc.sync.dma_start(out=g_sb[:, 2:4, :], in_=g_rows[:, 2:4, :])
        nc.sync.dma_start(out=xf_sb[:], in_=xf.rearrange("(p i) d -> p i d", i=ROW_TILES))

        identity = keep.tile([P, P], F32)
        masks.make_identity(nc, identity[:])

        one = keep.tile([P, 1], F32)
        nc.vector.memset(one[:], 1.0)
        unused_root = keep.tile([P, 1], F32)
        nc.scalar.activation(out=unused_root[:], in_=one[:], func=ACT.Abs_reciprocal_sqrt)

        rsqrt = keep.tile([P, PACK, D], F32)
        inv_var = keep.tile([P, PACK, D], F32)
        g_grouped = keep.tile([P, ROW_TILES, P, 2], F32, align_bytes=64)

        def copy_pair(pair):
            nc.scalar.copy(
                out=g_grouped[:, 2 * pair : 2 * pair + 2, :, :],
                in_=g_t[pair][:].rearrange("p j u n -> p j n u"),
            )

        def root(cols):
            nc.scalar.activation(out=rsqrt[:, :, cols], in_=var_sb[:, :, cols], func=ACT.Abs_reciprocal_sqrt)

        root(half_cols(0))
        root(half_cols(1))
        root(chunk_cols(1))
        for c in range(1, COL_CHUNKS):
            if c + 1 < COL_CHUNKS:
                root(chunk_cols(c + 1))
            cols = chunk_cols(c)
            nc.scalar.activation(out=inv_var[:, :, cols], in_=rsqrt[:, :, cols], func=ACT.Square)

        g_t = {}
        for pair in PAIR_ORDER:
            g_t[pair] = psum.tile([P, 2, 2, P], F32, tag="bank", name="g_t")
        unused_sums = psum.tile([P, WARM_COLS], F32, tag="bank")

        def transpose_pair(pair):
            for j in range(2):
                g_words = g_sb[:, 2 * pair + j, :].bitcast(F32).rearrange("n (p u) -> n u p", u=2)
                for u in range(2):
                    nc.tensor.transpose(g_t[pair][:, j, u, :], g_words[:, u, :], identity[:])

        def warm_up(values, c):
            first = COL_CHUNK * (c - 1)
            nc.tensor.matmul(
                out=unused_sums[:], lhsT=identity[:], rhs=values[:, 0, first : first + WARM_COLS],
                start=True, stop=True,
            )

        for c in (1, 2, 3):
            warm_up(rsqrt, c)
        transpose_pair(PAIR_ORDER[0])
        for c in (4, 5):
            warm_up(rsqrt, c)
        transpose_pair(PAIR_ORDER[1])
        for c in (6, 7):
            warm_up(rsqrt, c)
        for c in (6, 7):
            warm_up(inv_var, c)

        for pair in PAIR_ORDER:
            copy_pair(pair)

        iv_grouped = keep.tile([P, D, PACK], BF16, align_bytes=64)
        miv_grouped = keep.tile([P, D, PACK], BF16, align_bytes=64)
        iv_codes = keep.tile([P, D], U32, align_bytes=64)
        iv_scales = keep.tile([P, D], U8, align_bytes=64)
        miv_codes = keep.tile([P, D], U32, align_bytes=64)
        miv_scales = keep.tile([P, D], U8, align_bytes=64)
        g_codes = keep.tile([P, NT], U32, align_bytes=64)
        g_scales = keep.tile([P, NT], U8, align_bytes=64)

        def quantise_pair(pair):
            pair_rows = slice(2 * P * pair, 2 * P * (pair + 1))
            nc.vector.quantize_mx(
                out=g_codes[:, pair_rows].bitcast(E5M2_X4),
                scales=g_scales[:, pair_rows],
                in_=g_grouped[:, 2 * pair : 2 * pair + 2, :, :]
                .rearrange("p j n u -> p (j n u)")
                .bitcast(BF16),
            )

        def round_inv_var(cols):
            nc.vector.tensor_copy(out=by_word(iv_grouped, cols), in_=by_row(inv_var, cols))

        def mean_times_inv_var(cols):
            nc.vector.tensor_tensor(
                out=by_word(miv_grouped, cols), in0=by_row(mean_sb, cols), in1=by_row(inv_var, cols), op=ALU.mult
            )

        last = COL_CHUNKS - 1
        for h in range(2):
            cols = half_cols(h)
            nc.vector.tensor_tensor(
                out=inv_var[:, :, cols], in0=rsqrt[:, :, cols], in1=rsqrt[:, :, cols], op=ALU.mult
            )
        for h in range(2):
            round_inv_var(half_cols(h))
        for h in range(2):
            mean_times_inv_var(half_cols(h))
        for c in range(1, last):
            round_inv_var(chunk_cols(c))
            quantise_chunk(nc, iv_grouped, iv_codes, iv_scales, c - 1)
            mean_times_inv_var(chunk_cols(c))
            quantise_chunk(nc, miv_grouped, miv_codes, miv_scales, c - 1)
        round_inv_var(chunk_cols(last))
        quantise_chunk(nc, iv_grouped, iv_codes, iv_scales, last - 1)
        quantise_pair(PAIR_ORDER[0])
        quantise_chunk(nc, iv_grouped, iv_codes, iv_scales, last)
        mean_times_inv_var(chunk_cols(last))
        quantise_chunk(nc, miv_grouped, miv_codes, miv_scales, last - 1)
        quantise_pair(PAIR_ORDER[1])
        quantise_chunk(nc, miv_grouped, miv_codes, miv_scales, last)

        def mx_pass(i, codes, scales):
            rows = slice(P * i, P * (i + 1))
            sums = psum.tile([P, D], F32, tag="bank", name="sums")
            nc.tensor.matmul_mx(
                out=sums[:],
                lhsT=g_codes[:, rows].bitcast(E5M2_X4), lhsT_scale=g_scales[:, rows],
                rhs=codes[:].bitcast(E4M3_X4), rhs_scale=scales[:],
                start=True, stop=True,
            )
            return sums

        tile_order = [2 * pair + j for pair in PAIR_ORDER for j in range(2)]
        b_ps = {}
        xf_b = {}
        for i in tile_order:
            b_ps[i] = mx_pass(i, iv_codes, iv_scales)
            xf_b[i] = products.tile([P, D], F32, name="product")
        nc.vector.memset(xf_b[GPSIMD_TILES[0]][:, :1], 0.0)
        for i in GPSIMD_TILES:
            b_sb = copies.tile([P, D], F32, name="b_sb")
            nc.scalar.copy(out=b_sb[:], in_=b_ps[i][:])
            nc.gpsimd.tensor_tensor(out=xf_b[i][:], in0=b_sb[:], in1=xf_sb[:, i, :], op=ALU.mult)
        vector_tiles = [i for i in range(ROW_TILES) if i not in GPSIMD_TILES]
        end_order = vector_tiles + list(GPSIMD_TILES)
        a_ps = {}
        for i in end_order:
            a_ps[i] = mx_pass(i, miv_codes, miv_scales)

        out_sb = keep.tile([P, ROW_TILES, D], F32)
        out_rows = out.rearrange("(p i) d -> p i d", i=ROW_TILES)

        def vector_product(i):
            nc.vector.tensor_tensor(out=xf_b[i][:], in0=xf_sb[:, i, :], in1=b_ps[i][:], op=ALU.mult)

        for i in vector_tiles:
            vector_product(i)
        for i in end_order:
            pieces = LAST_PIECES if i == end_order[-1] else 1
            width = D // pieces
            for h in range(pieces):
                cols = slice(width * h, width * (h + 1))
                nc.vector.scalar_tensor_tensor(
                    out=out_sb[:, i, cols], in0=xf_b[i][:, cols], scalar=-1.0, in1=a_ps[i][:, cols],
                    op0=ALU.mult, op1=ALU.add,
                )
                nc.sync.dma_start(out=out_rows[:, i, cols], in_=out_sb[:, i, cols])
